import numpy as np
import ml_dtypes


def mxq(x, axis, fmt="e4m3"):
    dtype, down = {"e4m3": (ml_dtypes.float8_e4m3fn, 7), "e5m2": (ml_dtypes.float8_e5m2, 14)}[fmt]
    v = np.moveaxis(np.asarray(x, np.float32).astype(ml_dtypes.bfloat16).astype(np.float64), axis, -1)
    blocks = v.reshape(v.shape[:-1] + (-1, 32))
    amax = np.abs(blocks).max(-1, keepdims=True)
    byte = np.maximum(np.where(amax > 0, np.frexp(amax)[1] - 1 + 127, 0) - down, 1)
    scale = np.exp2(byte - 127.0)
    codes = (blocks / scale).astype(np.float32).astype(dtype).astype(np.float64)
    return np.moveaxis((codes * scale).reshape(v.shape), -1, axis)


WIDE = False


def mx_kscale(k):
    if not WIDE:
        return np.ones(k)
    levels = np.array([10, -10, 5, -5, 0])
    a = np.random.permutation(np.resize(levels, k // 512 * 4)).reshape(k // 512, 4)
    idx = np.arange(k)
    return np.exp2(a[idx // 512, idx % 128 // 32])


BF16 = ml_dtypes.bfloat16


def bf(x):
    return np.asarray(x, np.float32).astype(BF16)


def f64(x):
    return np.asarray(x).astype(np.float64)


T, H, NQ, NKV, HD = 8192, 1024, 2, 1, 64
RD = HD // 2
QS, KS = NQ * HD, NKV * HD
OUT = QS + 2 * KS


def extract_rope(x):
    r = x[..., :RD]
    r = r.reshape(*r.shape[:-1], RD // 2, 2)
    return np.swapaxes(r, -2, -1).reshape(*x.shape[:-1], RD)


def fill_rope(x, rope):
    r = rope.reshape(*rope.shape[:-1], 2, RD // 2)
    r = np.swapaxes(r, -2, -1).reshape(*rope.shape)
    return np.concatenate([r, x[..., RD:]], axis=-1)


def rotate_half(x):
    half = x.shape[-1] // 2
    return np.concatenate([-x[..., half:], x[..., :half]], axis=-1)


def setup_inputs():
    s = mx_kscale(H)
    ang = np.random.uniform(0.0, 2.0 * np.pi, (T, RD))
    return {'hidden_states': bf(np.random.standard_normal((T, H)) * s),
            'cos': bf(np.cos(ang)), 'sin': bf(np.sin(ang)),
            'W_qkv': bf(np.random.standard_normal((H, OUT)) / np.sqrt(H) / s[:, None]),
            'b_qkv': bf(np.random.standard_normal(OUT) * 0.3)}


def reference(hidden_states, cos, sin, W_qkv, b_qkv):
    qkv = (mxq(f64(hidden_states), 1, 'e4m3') @ mxq(f64(W_qkv), 0, 'e4m3')) + f64(b_qkv)
    q = qkv[:, :QS].reshape(T, NQ, HD)
    k = qkv[:, QS:QS + KS].reshape(T, NKV, HD)
    v = qkv[:, QS + KS:].reshape(T, NKV, HD)
    cos_b = f64(cos)[:, None, :]
    sin_b = f64(sin)[:, None, :]
    q_r = extract_rope(q)
    k_r = extract_rope(k)
    q_r = q_r * cos_b + rotate_half(q_r) * sin_b
    k_r = k_r * cos_b + rotate_half(k_r) * sin_b
    q = fill_rope(q, q_r)
    k = fill_rope(k, k_r)
    return q, k, v

@@ -1,0 +1,259 @@
+from contextlib import ExitStack
+
+import concourse.mybir as mybir
+from concourse.masks import make_identity
+
+F32 = mybir.dt.float32
+BF16 = mybir.dt.bfloat16
+U32 = mybir.dt.uint32
+U8 = mybir.dt.uint8
+FP8X4 = mybir.dt.float8_e4m3fn_x4
+ALU = mybir.AluOpType
+
+P = 128
+T, H, OUT = 8192, 1024, 256
+NT = T // P
+FLOPS = 2 * T * H * OUT
+
+ROUNDS = [1, 1, 2] + [4] * 15
+GROUPS = [[0, 1, 2]] + [[3 + 2 * g, 4 + 2 * g] for g in range(7)] + [[17]]
+XB = 8
+RMAX = 4
+GMAX = 8
+
+
+def tile_selfattention_pa_t_kernel(tc, hidden_states, cos, sin, W_qkv, b_qkv, out_0, out_1, out_2):
+    nc = tc.nc
+    nr = len(ROUNDS)
+    first = [sum(ROUNDS[:r]) for r in range(nr)]
+    group_of = {}
+    for g, rs in enumerate(GROUPS):
+        for r in rs:
+            group_of[r] = g
+    x_v = hidden_states.rearrange("(p i) k -> p i k", i=NT)
+    q_v = out_0.rearrange("(p i) h d -> p i (h d)", i=NT)
+    k_v = out_1.rearrange("(p i) h d -> p i (h d)", i=NT)
+    v_v = out_2.rearrange("(p i) h d -> p i (h d)", i=NT)
+
+    with ExitStack() as ctx:
+        ctx.enter_context(tc.manual_schedule())
+        const = ctx.enter_context(tc.tile_pool(name="const", bufs=1))
+        xpool = ctx.enter_context(tc.tile_pool(name="xpool", bufs=XB))
+        gpool = ctx.enter_context(tc.tile_pool(name="gpool", bufs=3))
+        opool = ctx.enter_context(tc.tile_pool(name="opool", bufs=3))
+        spool = ctx.enter_context(tc.tile_pool(name="spool", bufs=2))
+        tp = ctx.enter_context(tc.psum_pool(name="tp", bufs=4))
+        mm = ctx.enter_context(tc.psum_pool(name="mm", bufs=2))
+
+        x_t, xt_t, grp_t, codes_t, scl_t, pq_t, pkv_t, o_t = {}, {}, {}, {}, {}, {}, {}, {}
+
+        def load(r):
+            nt = ROUNDS[r]
+            xc = xpool.tile([P, RMAX * H], BF16)
+            nc.sync.dma_start(
+                out=xc[:, 0 : nt * H].rearrange("p (n k) -> p n k", k=H),
+                in_=x_v[:, first[r] : first[r] + nt, :],
+            )
+            x_t[r] = xc
+
+        def transp(r):
+            xw = x_t[r][:].bitcast(F32)
+            xt_t[r] = []
+            for a in range(ROUNDS[r]):
+                xt = tp.tile([P, 4, P], F32)
+                for b in range(4):
+                    w0 = a * 512 + b * P
+                    nc.tensor.transpose(xt[:, b, :], xw[:, w0 : w0 + P], ident[:])
+                xt_t[r].append(xt)
+
+        def copyout(r):
+            grp = gpool.tile([P, RMAX * H], BF16, align_bytes=64)
+            gw = grp[:].bitcast(F32)
+            for a in range(ROUNDS[r]):
+                nc.scalar.copy(
+                    out=gw[:, a * 512 : (a + 1) * 512].rearrange("p (g m u) -> p g m u", g=2, u=2),
+                    in_=xt_t[r][a][:].rearrange("p (g u) m -> p g m u", u=2),
+                )
+            grp_t[r] = grp
+
+        def quant(r):
+            nt = ROUNDS[r]
+            codes = gpool.tile([P, RMAX * 256], U32, align_bytes=64)
+            scl = gpool.tile([P, RMAX * 256], U8, align_bytes=64)
+            nc.vector.quantize_mx(
+                out=codes[:, 0 : nt * 256].bitcast(FP8X4),
+                scales=scl[:, 0 : nt * 256],
+                in_=grp_t[r][:, 0 : nt * H],
+            )
+            codes_t[r] = codes
+            scl_t[r] = scl
+
+        def mx(r):
+            pq = mm.tile([P, RMAX, P], F32)
+            pkv = mm.tile([P, RMAX, P], F32)
+            for a in range(ROUNDS[r]):
+                for ps, c0 in ((pq, 0), (pkv, P)):
+                    for g in range(2):
+                        s0 = a * 256 + g * P
+                        nc.tensor.matmul_mx(
+                            out=ps[:, a, :],
+                            lhsT=codes_t[r][:, s0 : s0 + P].bitcast(FP8X4),
+                            lhsT_scale=scl_t[r][:, s0 : s0 + P],
+                            rhs=w_codes[g][:, c0 : c0 + P].bitcast(FP8X4),
+                            rhs_scale=w_scl[g][:, c0 : c0 + P],
+                            start=(g == 0),
+                            stop=(g == 1),
+                        )
+            pq_t[r] = pq
+            pkv_t[r] = pkv
+
+        def bias_add(r):
+            g = group_of[r]
+            nt = ROUNDS[r]
+            gn = sum([ROUNDS[j] for j in GROUPS[g]])
+            n0 = first[r] - first[GROUPS[g][0]]
+            if r == GROUPS[g][0]:
+                o = opool.tile([P, GMAX * OUT], F32)
+                o_t[g] = o
+            o = o_t[g]
+            nc.vector.tensor_tensor(
+                out=o[:, n0 * P : (n0 + nt) * P].rearrange("p (n c) -> p n c", c=P),
+                in0=pq_t[r][:, 0:nt, :],
+                in1=b_bc[:, 0:P].unsqueeze(1).to_broadcast([P, nt, P]),
+                op=ALU.add,
+            )
+            nc.vector.tensor_tensor(
+                out=o[:, gn * P : gn * OUT].rearrange("p (s n c) -> p n s c", s=2, c=64)[:, n0 : n0 + nt],
+                in0=pkv_t[r][:, 0:nt, :].rearrange("p n (s c) -> p n s c", s=2),
+                in1=b_bc[:, P:OUT].rearrange("p (s c) -> p s c", s=2).unsqueeze(1).to_broadcast([P, nt, 2, 64]),
+                op=ALU.add,
+            )
+
+        def rope(g):
+            gn = sum([ROUNDS[j] for j in GROUPS[g]])
+            i0 = first[GROUPS[g][0]]
+            o = o_t[g]
+            cosv = cos_sb[:].rearrange("p (i c) -> p i c", c=32)[:, i0 : i0 + gn, :]
+            sinv = sin_sb[:].rearrange("p (i c) -> p i c", c=32)[:, i0 : i0 + gn, :]
+            t1q = spool.tile([P, GMAX * 64], F32)
+            t2q = spool.tile([P, GMAX * 64], F32)
+            t1k = spool.tile([P, GMAX * 32], F32)
+            t2k = spool.tile([P, GMAX * 32], F32)
+            xq = o[:, 0 : gn * P].rearrange("p (n h d) -> p n h d", h=2, d=64)
+            xk = o[:, gn * P : gn * 192].rearrange("p (n d) -> p n d", d=64)
+            t1qv = t1q[:, 0 : gn * 64].rearrange("p (n h c) -> p n h c", h=2, c=32)
+            t2qv = t2q[:, 0 : gn * 64].rearrange("p (n h c) -> p n h c", h=2, c=32)
+            t1kv = t1k[:, 0 : gn * 32].rearrange("p (n c) -> p n c", c=32)
+            t2kv = t2k[:, 0 : gn * 32].rearrange("p (n c) -> p n c", c=32)
+            nc.vector.tensor_tensor(
+                out=t1qv, in0=xq[:, :, :, 0:32], in1=cosv.unsqueeze(2).to_broadcast([P, gn, 2, 32]), op=ALU.mult
+            )
+            for e in range(2):
+                lo, ot = 16 * e, 16 * (1 - e)
+                nc.vector.tensor_tensor(
+                    out=t2qv[:, :, :, lo : lo + 16],
+                    in0=xq[:, :, :, ot : ot + 16],
+                    in1=sinv[:, :, lo : lo + 16].unsqueeze(2).to_broadcast([P, gn, 2, 16]),
+                    op=ALU.mult,
+                )
+            nc.vector.tensor_tensor(out=t1kv, in0=xk[:, :, 0:32], in1=cosv, op=ALU.mult)
+            for e in range(2):
+                lo, ot = 16 * e, 16 * (1 - e)
+                nc.vector.tensor_tensor(
+                    out=t2kv[:, :, lo : lo + 16], in0=xk[:, :, ot : ot + 16], in1=sinv[:, :, lo : lo + 16], op=ALU.mult
+                )
+            nc.vector.tensor_tensor(
+                out=o[:, 0 : gn * P].rearrange("p (u d) -> p u d", d=64)[:, :, 0:32].rearrange("p u (j e) -> p u j e", e=2),
+                in0=t1q[:, 0 : gn * 64].rearrange("p (u e j) -> p u j e", e=2, j=16),
+                in1=t2q[:, 0 : gn * 64].rearrange("p (u e j) -> p u j e", e=2, j=16),
+                op=ALU.add,
+            )
+            nc.vector.tensor_tensor(
+                out=xk[:, :, 0:32].rearrange("p u (j e) -> p u j e", e=2),
+                in0=t1k[:, 0 : gn * 32].rearrange("p (u e j) -> p u j e", e=2, j=16),
+                in1=t2k[:, 0 : gn * 32].rearrange("p (u e j) -> p u j e", e=2, j=16),
+                op=ALU.add,
+            )
+
+        def store(g):
+            gn = sum([ROUNDS[j] for j in GROUPS[g]])
+            i0 = first[GROUPS[g][0]]
+            o = o_t[g]
+            nc.sync.dma_start(out=q_v[:, i0 : i0 + gn, :], in_=o[:, 0 : gn * P].rearrange("p (n c) -> p n c", c=P))
+            nc.sync.dma_start(
+                out=k_v[:, i0 : i0 + gn, :], in_=o[:, gn * P : gn * 192].rearrange("p (n c) -> p n c", c=64)
+            )
+            nc.sync.dma_start(
+                out=v_v[:, i0 : i0 + gn, :], in_=o[:, gn * 192 : gn * OUT].rearrange("p (n c) -> p n c", c=64)
+            )
+
+        ident = const.tile([P, P], F32)
+        make_identity(nc, ident[:])
+        b_row = const.tile([P, OUT], BF16)
+        nc.vector.memset(b_row[:], 0.0)
+        ones = const.tile([P, P], BF16)
+        nc.vector.memset(ones[:], 1.0)
+
+        w_raw = const.tile([P, 2 * 4 * OUT], BF16)
+        nc.scalar.dma_start(
+            out=w_raw[:].rearrange("p (a f) -> p a f", a=4),
+            in_=W_qkv.rearrange("(a p e) c -> p a (e c)", a=4, e=2),
+        )
+        load(0)
+        nc.scalar.dma_start(out=b_row[0:1, :], in_=b_qkv.rearrange("(o c) -> o c", o=1))
+        sin_sb = const.tile([P, NT * 32], BF16)
+        nc.scalar.dma_start(out=sin_sb[:], in_=sin.rearrange("(p i) c -> p (i c)", i=NT))
+        cos_sb = const.tile([P, NT * 32], BF16)
+        nc.scalar.dma_start(out=cos_sb[:], in_=cos.rearrange("(p i) c -> p (i c)", i=NT))
+        for r in range(1, XB):
+            load(r)
+
+        sneg = sin_sb[:].rearrange("p (i e j) -> p i e j", e=2, j=16)[:, :, 0, :]
+        nc.gpsimd.tensor_scalar(out=sneg, in0=sneg, scalar1=-1.0, scalar2=0.0, op0=ALU.mult, op1=ALU.add)
+
+        w_codes, w_scl = [], []
+        for g in range(2):
+            w_grp = const.tile([P, OUT * 4], BF16, name="w_grp%d" % g, align_bytes=64)
+            src = w_raw[:, g * 1024 : (g + 1) * 1024].rearrange("p (t n m) -> p n m t", t=4, n=4)
+            dst = w_grp[:].rearrange("p (n m t) -> p n m t", n=4, t=4)
+            for e in range(2):
+                nc.vector.tensor_copy(out=dst[:, 0:3, 16 * e : 16 * e + 16, :], in_=src[:, 0:3, e:32:2, :])
+            nc.vector.tensor_copy(out=dst[:, 0:3, 32:64, :], in_=src[:, 0:3, 32:64, :])
+            nc.vector.tensor_copy(out=dst[:, 3, :, :], in_=src[:, 3, :, :])
+            wc = const.tile([P, OUT], U32, name="w_codes%d" % g, align_bytes=64)
+            ws = const.tile([P, OUT], U8, name="w_scl%d" % g, align_bytes=64)
+            nc.vector.quantize_mx(out=wc[:].bitcast(FP8X4), scales=ws[:], in_=w_grp[:])
+            w_codes.append(wc)
+            w_scl.append(ws)
+
+        for r in range(3):
+            transp(r)
+            load(r + XB)
+            copyout(r)
+
+        pb = mm.tile([P, RMAX, P], F32, tag="pq")
+        pb2 = pb[:].rearrange("p a c -> p (a c)")[:, 0:OUT]
+        nc.tensor.matmul(out=pb2, lhsT=ones[:], rhs=b_row[:], start=True, stop=True)
+        b_bc = const.tile([P, OUT], F32)
+        pbv = pb2.rearrange("p (n m) -> p n m", n=4)
+        bbv = b_bc[:].rearrange("p (n m) -> p n m", n=4)
+        for e in range(2):
+            nc.scalar.copy(out=bbv[:, 0:3, 16 * e : 16 * e + 16], in_=pbv[:, 0:3, e:32:2])
+        nc.scalar.copy(out=bbv[:, 0:3, 32:64], in_=pbv[:, 0:3, 32:64])
+        nc.scalar.copy(out=bbv[:, 3, :], in_=pbv[:, 3, :])
+
+        quant(0)
+        for r in range(nr):
+            mx(r)
+            if 3 <= r + 2 < nr:
+                transp(r + 2)
+                if r + 2 + XB < nr:
+                    load(r + 2 + XB)
+                copyout(r + 2)
+            if r + 1 < nr:
+                quant(r + 1)
+            bias_add(r)
+            g = group_of[r]
+            if r == GROUPS[g][-1]:
+                rope(g)
+                store(g)

@@ -15,9 +15,9 @@ T, H, OUT = 8192, 1024, 256
 NT = T // P
 FLOPS = 2 * T * H * OUT
 
-ROUNDS = [1, 1, 2] + [4] * 15
-GROUPS = [[0, 1, 2]] + [[3 + 2 * g, 4 + 2 * g] for g in range(7)] + [[17]]
-XB = 8
+ROUNDS = [1, 1, 2] + [4] * 14 + [2, 2]
+GROUPS = [[0, 1, 2]] + [[3 + 2 * g, 4 + 2 * g] for g in range(7)] + [[17], [18]]
+XB = 10
 RMAX = 4
 GMAX = 8
 
@@ -39,7 +39,7 @@ def tile_selfattention_pa_t_kernel(tc, hidden_states, cos, sin, W_qkv, b_qkv, ou
         ctx.enter_context(tc.manual_schedule())
         const = ctx.enter_context(tc.tile_pool(name="const", bufs=1))
         xpool = ctx.enter_context(tc.tile_pool(name="xpool", bufs=XB))
-        gpool = ctx.enter_context(tc.tile_pool(name="gpool", bufs=3))
+        gpool = ctx.enter_context(tc.tile_pool(name="gpool", bufs=4))
         opool = ctx.enter_context(tc.tile_pool(name="opool", bufs=3))
         spool = ctx.enter_context(tc.tile_pool(name="spool", bufs=2))
         tp = ctx.enter_context(tc.psum_pool(name="tp", bufs=4))
@@ -243,15 +243,16 @@ def tile_selfattention_pa_t_kernel(tc, hidden_states, cos, sin, W_qkv, b_qkv, ou
         nc.scalar.copy(out=bbv[:, 3, :], in_=pbv[:, 3, :])
 
         quant(0)
+        quant(1)
         for r in range(nr):
             mx(r)
-            if 3 <= r + 2 < nr:
-                transp(r + 2)
-                if r + 2 + XB < nr:
-                    load(r + 2 + XB)
-                copyout(r + 2)
-            if r + 1 < nr:
-                quant(r + 1)
+            if r + 3 < nr:
+                transp(r + 3)
+                if r + 3 + XB < nr:
+                    load(r + 3 + XB)
+                copyout(r + 3)
+            if r + 2 < nr:
+                quant(r + 2)
             bias_add(r)
             g = group_of[r]
             if r == GROUPS[g][-1]:

@@ -15,8 +15,12 @@ T, H, OUT = 8192, 1024, 256
 NT = T // P
 FLOPS = 2 * T * H * OUT
 
-ROUNDS = [1, 1, 2] + [4] * 14 + [2, 2]
-GROUPS = [[0, 1, 2]] + [[3 + 2 * g, 4 + 2 * g] for g in range(7)] + [[17], [18]]
+ROUNDS = [1, 1, 2, 4] + [4] * 12 + [4, 2, 2]
+GROUPS = [[0], [1], [2], [3]] + [[4 + 2 * g, 5 + 2 * g] for g in range(6)] + [[16], [17], [18]]
+GP_ADD = range(4, 10)
+SC_PARTS = [(0, 24), (24, 64)]
+HEAD = ["x0", "x1", "x2", "x3", "sc0", "x4", "x5", "x6", "x7", "x8", "sc1", "x9"]
+LT = 3
 XB = 10
 RMAX = 4
 GMAX = 8
@@ -40,7 +44,7 @@ def tile_selfattention_pa_t_kernel(tc, hidden_states, cos, sin, W_qkv, b_qkv, ou
         const = ctx.enter_context(tc.tile_pool(name="const", bufs=1))
         xpool = ctx.enter_context(tc.tile_pool(name="xpool", bufs=XB))
         gpool = ctx.enter_context(tc.tile_pool(name="gpool", bufs=4))
-        opool = ctx.enter_context(tc.tile_pool(name="opool", bufs=3))
+        opool = ctx.enter_context(tc.tile_pool(name="opool", bufs=4))
         spool = ctx.enter_context(tc.tile_pool(name="spool", bufs=2))
         tp = ctx.enter_context(tc.psum_pool(name="tp", bufs=4))
         mm = ctx.enter_context(tc.psum_pool(name="mm", bufs=2))
@@ -162,13 +166,14 @@ def tile_selfattention_pa_t_kernel(tc, hidden_states, cos, sin, W_qkv, b_qkv, ou
                 nc.vector.tensor_tensor(
                     out=t2kv[:, :, lo : lo + 16], in0=xk[:, :, ot : ot + 16], in1=sinv[:, :, lo : lo + 16], op=ALU.mult
                 )
-            nc.vector.tensor_tensor(
+            add_eng = nc.gpsimd if g in GP_ADD else nc.vector
+            add_eng.tensor_tensor(
                 out=o[:, 0 : gn * P].rearrange("p (u d) -> p u d", d=64)[:, :, 0:32].rearrange("p u (j e) -> p u j e", e=2),
                 in0=t1q[:, 0 : gn * 64].rearrange("p (u e j) -> p u j e", e=2, j=16),
                 in1=t2q[:, 0 : gn * 64].rearrange("p (u e j) -> p u j e", e=2, j=16),
                 op=ALU.add,
             )
-            nc.vector.tensor_tensor(
+            add_eng.tensor_tensor(
                 out=xk[:, :, 0:32].rearrange("p u (j e) -> p u j e", e=2),
                 in0=t1k[:, 0 : gn * 32].rearrange("p (u e j) -> p u j e", e=2, j=16),
                 in1=t2k[:, 0 : gn * 32].rearrange("p (u e j) -> p u j e", e=2, j=16),
@@ -179,11 +184,11 @@ def tile_selfattention_pa_t_kernel(tc, hidden_states, cos, sin, W_qkv, b_qkv, ou
             gn = sum([ROUNDS[j] for j in GROUPS[g]])
             i0 = first[GROUPS[g][0]]
             o = o_t[g]
-            nc.sync.dma_start(out=q_v[:, i0 : i0 + gn, :], in_=o[:, 0 : gn * P].rearrange("p (n c) -> p n c", c=P))
-            nc.sync.dma_start(
+            nc.scalar.dma_start(out=q_v[:, i0 : i0 + gn, :], in_=o[:, 0 : gn * P].rearrange("p (n c) -> p n c", c=P))
+            nc.scalar.dma_start(
                 out=k_v[:, i0 : i0 + gn, :], in_=o[:, gn * P : gn * 192].rearrange("p (n c) -> p n c", c=64)
             )
-            nc.sync.dma_start(
+            nc.scalar.dma_start(
                 out=v_v[:, i0 : i0 + gn, :], in_=o[:, gn * 192 : gn * OUT].rearrange("p (n c) -> p n c", c=64)
             )
 
@@ -194,42 +199,23 @@ def tile_selfattention_pa_t_kernel(tc, hidden_states, cos, sin, W_qkv, b_qkv, ou
         ones = const.tile([P, P], BF16)
         nc.vector.memset(ones[:], 1.0)
 
+        nc.sync.dma_start(out=b_row[0:1, :], in_=b_qkv.rearrange("(o c) -> o c", o=1))
         w_raw = const.tile([P, 2 * 4 * OUT], BF16)
-        nc.scalar.dma_start(
+        nc.sync.dma_start(
             out=w_raw[:].rearrange("p (a f) -> p a f", a=4),
             in_=W_qkv.rearrange("(a p e) c -> p a (e c)", a=4, e=2),
         )
-        load(0)
-        nc.scalar.dma_start(out=b_row[0:1, :], in_=b_qkv.rearrange("(o c) -> o c", o=1))
         sin_sb = const.tile([P, NT * 32], BF16)
-        nc.scalar.dma_start(out=sin_sb[:], in_=sin.rearrange("(p i) c -> p (i c)", i=NT))
         cos_sb = const.tile([P, NT * 32], BF16)
-        nc.scalar.dma_start(out=cos_sb[:], in_=cos.rearrange("(p i) c -> p (i c)", i=NT))
-        for r in range(1, XB):
-            load(r)
-
-        sneg = sin_sb[:].rearrange("p (i e j) -> p i e j", e=2, j=16)[:, :, 0, :]
-        nc.gpsimd.tensor_scalar(out=sneg, in0=sneg, scalar1=-1.0, scalar2=0.0, op0=ALU.mult, op1=ALU.add)
-
-        w_codes, w_scl = [], []
-        for g in range(2):
-            w_grp = const.tile([P, OUT * 4], BF16, name="w_grp%d" % g, align_bytes=64)
-            src = w_raw[:, g * 1024 : (g + 1) * 1024].rearrange("p (t n m) -> p n m t", t=4, n=4)
-            dst = w_grp[:].rearrange("p (n m t) -> p n m t", n=4, t=4)
-            for e in range(2):
-                nc.vector.tensor_copy(out=dst[:, 0:3, 16 * e : 16 * e + 16, :], in_=src[:, 0:3, e:32:2, :])
-            nc.vector.tensor_copy(out=dst[:, 0:3, 32:64, :], in_=src[:, 0:3, 32:64, :])
-            nc.vector.tensor_copy(out=dst[:, 3, :, :], in_=src[:, 3, :, :])
-            wc = const.tile([P, OUT], U32, name="w_codes%d" % g, align_bytes=64)
-            ws = const.tile([P, OUT], U8, name="w_scl%d" % g, align_bytes=64)
-            nc.vector.quantize_mx(out=wc[:].bitcast(FP8X4), scales=ws[:], in_=w_grp[:])
-            w_codes.append(wc)
-            w_scl.append(ws)
-
-        for r in range(3):
-            transp(r)
-            load(r + XB)
-            copyout(r)
+        sin_v = sin.rearrange("(p i) c -> p (i c)", i=NT)
+        cos_v = cos.rearrange("(p i) c -> p (i c)", i=NT)
+        for item in HEAD:
+            if item[0] == "x":
+                load(int(item[1:]))
+            else:
+                lo, hi = SC_PARTS[int(item[2:])]
+                nc.sync.dma_start(out=sin_sb[:, lo * 32 : hi * 32], in_=sin_v[:, lo * 32 : hi * 32])
+                nc.sync.dma_start(out=cos_sb[:, lo * 32 : hi * 32], in_=cos_v[:, lo * 32 : hi * 32])
 
         pb = mm.tile([P, RMAX, P], F32, tag="pq")
         pb2 = pb[:].rearrange("p a c -> p (a c)")[:, 0:OUT]
@@ -242,19 +228,54 @@ def tile_selfattention_pa_t_kernel(tc, hidden_states, cos, sin, W_qkv, b_qkv, ou
         nc.scalar.copy(out=bbv[:, 0:3, 32:64], in_=pbv[:, 0:3, 32:64])
         nc.scalar.copy(out=bbv[:, 3, :], in_=pbv[:, 3, :])
 
-        quant(0)
-        quant(1)
-        for r in range(nr):
-            mx(r)
-            if r + 3 < nr:
-                transp(r + 3)
-                if r + 3 + XB < nr:
-                    load(r + 3 + XB)
-                copyout(r + 3)
-            if r + 2 < nr:
-                quant(r + 2)
-            bias_add(r)
-            g = group_of[r]
-            if r == GROUPS[g][-1]:
-                rope(g)
-                store(g)
+        w_codes, w_scl = [], []
+
+        def w_prep():
+            for g in range(2):
+                w_grp = const.tile([P, OUT * 4], BF16, name="w_grp%d" % g, align_bytes=64)
+                src = w_raw[:, g * 1024 : (g + 1) * 1024].rearrange("p (t n m) -> p n m t", t=4, n=4)
+                dst = w_grp[:].rearrange("p (n m t) -> p n m t", n=4, t=4)
+                for e in range(2):
+                    nc.vector.tensor_copy(out=dst[:, 0:3, 16 * e : 16 * e + 16, :], in_=src[:, 0:3, e:32:2, :])
+                nc.vector.tensor_copy(out=dst[:, 0:3, 32:64, :], in_=src[:, 0:3, 32:64, :])
+                nc.vector.tensor_copy(out=dst[:, 3, :, :], in_=src[:, 3, :, :])
+                wc = const.tile([P, OUT], U32, name="w_codes%d" % g, align_bytes=64)
+                ws = const.tile([P, OUT], U8, name="w_scl%d" % g, align_bytes=64)
+                nc.vector.quantize_mx(out=wc[:].bitcast(FP8X4), scales=ws[:], in_=w_grp[:])
+                w_codes.append(wc)
+                w_scl.append(ws)
+
+        negated = []
+
+        def negate_sin(g):
+            i0 = first[GROUPS[g][0]]
+            for part, (lo, hi) in enumerate(SC_PARTS):
+                if lo <= i0 < hi and part not in negated:
+                    negated.append(part)
+                    sneg = sin_sb[:, lo * 32 : hi * 32].rearrange("p (i e j) -> p i e j", e=2, j=16)[:, :, 0, :]
+                    nc.vector.tensor_scalar_mul(out=sneg, in0=sneg, scalar1=-1.0)
+
+        ng = len(GROUPS)
+        for g in range(-LT, ng + 1):
+            if g == -1:
+                w_prep()
+            if 0 <= g + 1 < ng:
+                for r in GROUPS[g + 1]:
+                    quant(r)
+            if 0 <= g - 1 < ng:
+                negate_sin(g - 1)
+                rope(g - 1)
+            if 0 <= g < ng:
+                for r in GROUPS[g]:
+                    bias_add(r)
+            if 0 <= g + 1 < ng:
+                for r in GROUPS[g + 1]:
+                    mx(r)
+            if 0 <= g + LT < ng:
+                for r in GROUPS[g + LT]:
+                    transp(r)
+                    if r + XB < nr:
+                        load(r + XB)
+                    copyout(r)
+            if 0 <= g - 1 < ng:
+                store(g - 1)

@@ -9,21 +9,20 @@ U32 = mybir.dt.uint32
 U8 = mybir.dt.uint8
 FP8X4 = mybir.dt.float8_e4m3fn_x4
 ALU = mybir.AluOpType
+ACT = mybir.ActivationFunctionType
 
 P = 128
 T, H, OUT = 8192, 1024, 256
 NT = T // P
 FLOPS = 2 * T * H * OUT
 
-ROUNDS = [1, 1, 2, 4] + [4] * 12 + [4, 2, 2]
-GROUPS = [[0], [1], [2], [3]] + [[4 + 2 * g, 5 + 2 * g] for g in range(6)] + [[16], [17], [18]]
-GP_ADD = range(4, 10)
-SC_PARTS = [(0, 24), (24, 64)]
-HEAD = ["x0", "x1", "x2", "x3", "sc0", "x4", "x5", "x6", "x7", "x8", "sc1", "x9"]
-LT = 3
-XB = 10
+ROUNDS = [2, 2] + [4] * 14 + [2, 2]
+GROUPS = [[0, 1]] + [[2 + 2 * g, 3 + 2 * g] for g in range(7)] + [[16], [17]]
+HEAD = ["x0", "x1", "x2", "x3", "sc", "x4", "x5", "x6", "x7"]
+XB = 8
 RMAX = 4
 GMAX = 8
+KU_ON_SCALAR = True
 
 
 def tile_selfattention_pa_t_kernel(tc, hidden_states, cos, sin, W_qkv, b_qkv, out_0, out_1, out_2):
@@ -46,10 +45,15 @@ def tile_selfattention_pa_t_kernel(tc, hidden_states, cos, sin, W_qkv, b_qkv, ou
         gpool = ctx.enter_context(tc.tile_pool(name="gpool", bufs=4))
         opool = ctx.enter_context(tc.tile_pool(name="opool", bufs=4))
         spool = ctx.enter_context(tc.tile_pool(name="spool", bufs=2))
-        tp = ctx.enter_context(tc.psum_pool(name="tp", bufs=4))
-        mm = ctx.enter_context(tc.psum_pool(name="mm", bufs=2))
+        ps_x = ctx.enter_context(tc.psum_pool(name="ps_x", bufs=4))
+        ps_n = ctx.enter_context(tc.psum_pool(name="ps_n", bufs=1))
+        ps_t = ctx.enter_context(tc.psum_pool(name="ps_t", bufs=1))
+        ps_b = ctx.enter_context(tc.psum_pool(name="ps_b", bufs=2))
 
-        x_t, xt_t, grp_t, codes_t, scl_t, pq_t, pkv_t, o_t = {}, {}, {}, {}, {}, {}, {}, {}
+        x_t, xt_t, grp_t, codes_t, scl_t, pn_t, pt_t, xr_t, pb_t, o_t, t1_t, t2_t = {}, {}, {}, {}, {}, {}, {}, {}, {}, {}, {}, {}
+
+        def gsize(g):
+            return sum([ROUNDS[j] for j in GROUPS[g]])
 
         def load(r):
             nt = ROUNDS[r]
@@ -64,20 +68,18 @@ def tile_selfattention_pa_t_kernel(tc, hidden_states, cos, sin, W_qkv, b_qkv, ou
             xw = x_t[r][:].bitcast(F32)
             xt_t[r] = []
             for a in range(ROUNDS[r]):
-                xt = tp.tile([P, 4, P], F32)
+                xt = ps_x.tile([P, 4, P], F32)
                 for b in range(4):
                     w0 = a * 512 + b * P
                     nc.tensor.transpose(xt[:, b, :], xw[:, w0 : w0 + P], ident[:])
                 xt_t[r].append(xt)
 
         def copyout(r):
+            nt = ROUNDS[r]
             grp = gpool.tile([P, RMAX * H], BF16, align_bytes=64)
-            gw = grp[:].bitcast(F32)
-            for a in range(ROUNDS[r]):
-                nc.scalar.copy(
-                    out=gw[:, a * 512 : (a + 1) * 512].rearrange("p (g m u) -> p g m u", g=2, u=2),
-                    in_=xt_t[r][a][:].rearrange("p (g u) m -> p g m u", u=2),
-                )
+            gw = grp[:].bitcast(F32)[:, 0 : nt * 512].rearrange("p (g a m u) -> p g a m u", g=2, a=nt, u=2)
+            for a in range(nt):
+                nc.scalar.copy(out=gw[:, :, a], in_=xt_t[r][a][:].rearrange("p (g u) m -> p g m u", u=2))
             grp_t[r] = grp
 
         def quant(r):
@@ -93,102 +95,125 @@ def tile_selfattention_pa_t_kernel(tc, hidden_states, cos, sin, W_qkv, b_qkv, ou
             scl_t[r] = scl
 
         def mx(r):
-            pq = mm.tile([P, RMAX, P], F32)
-            pkv = mm.tile([P, RMAX, P], F32)
+            nt = ROUNDS[r]
+            w = nt * P
+            pt = ps_t.tile([P, RMAX * P], F32)
+            for g in range(2):
+                nc.tensor.matmul_mx(
+                    out=pt[:, 0:w],
+                    lhsT=w_codes[g][:, 0:P].bitcast(FP8X4),
+                    lhsT_scale=w_scl[g][:, 0:P],
+                    rhs=codes_t[r][:, g * w : (g + 1) * w].bitcast(FP8X4),
+                    rhs_scale=scl_t[r][:, g * w : (g + 1) * w],
+                    start=(g == 0),
+                    stop=(g == 1),
+                )
+            pn = ps_n.tile([P, RMAX, P], F32)
+            for a in range(nt):
+                for g in range(2):
+                    s0 = g * w + a * P
+                    nc.tensor.matmul_mx(
+                        out=pn[:, a, :],
+                        lhsT=codes_t[r][:, s0 : s0 + P].bitcast(FP8X4),
+                        lhsT_scale=scl_t[r][:, s0 : s0 + P],
+                        rhs=w_codes[g][:, P:OUT].bitcast(FP8X4),
+                        rhs_scale=w_scl[g][:, P:OUT],
+                        start=(g == 0),
+                        stop=(g == 1),
+                    )
+            pt_t[r] = pt
+            pn_t[r] = pn
+
+        def evac(r):
+            w = ROUNDS[r] * P
+            xr = spool.tile([P, RMAX * P], F32)
+            nc.scalar.activation(out=xr[:, 0:w], in_=pt_t[r][:, 0:w], func=ACT.Identity, bias=b_col[:, 0:1], scale=1.0)
+            xr_t[r] = xr
+
+        def tback(r):
+            pb = ps_b.tile([P, RMAX, P], F32)
             for a in range(ROUNDS[r]):
-                for ps, c0 in ((pq, 0), (pkv, P)):
-                    for g in range(2):
-                        s0 = a * 256 + g * P
-                        nc.tensor.matmul_mx(
-                            out=ps[:, a, :],
-                            lhsT=codes_t[r][:, s0 : s0 + P].bitcast(FP8X4),
-                            lhsT_scale=scl_t[r][:, s0 : s0 + P],
-                            rhs=w_codes[g][:, c0 : c0 + P].bitcast(FP8X4),
-                            rhs_scale=w_scl[g][:, c0 : c0 + P],
-                            start=(g == 0),
-                            stop=(g == 1),
-                        )
-            pq_t[r] = pq
-            pkv_t[r] = pkv
+                nc.tensor.transpose(pb[:, a, :], xr_t[r][:, a * P : (a + 1) * P], ident[:])
+            pb_t[r] = pb
 
         def bias_add(r):
             g = group_of[r]
             nt = ROUNDS[r]
-            gn = sum([ROUNDS[j] for j in GROUPS[g]])
+            gn = gsize(g)
             n0 = first[r] - first[GROUPS[g][0]]
             if r == GROUPS[g][0]:
                 o = opool.tile([P, GMAX * OUT], F32)
                 o_t[g] = o
             o = o_t[g]
             nc.vector.tensor_tensor(
-                out=o[:, n0 * P : (n0 + nt) * P].rearrange("p (n c) -> p n c", c=P),
-                in0=pq_t[r][:, 0:nt, :],
-                in1=b_bc[:, 0:P].unsqueeze(1).to_broadcast([P, nt, P]),
+                out=o[:, 0 : gn * P].rearrange("p (n h d) -> p n h d", h=2, d=64)[:, n0 : n0 + nt, :, 32:64],
+                in0=pn_t[r][:, 0:nt, 0:64].rearrange("p n (h c) -> p n h c", h=2),
+                in1=bb_nr[:, 0:64].rearrange("p (h c) -> p h c", h=2).unsqueeze(1).to_broadcast([P, nt, 2, 32]),
                 op=ALU.add,
             )
             nc.vector.tensor_tensor(
-                out=o[:, gn * P : gn * OUT].rearrange("p (s n c) -> p n s c", s=2, c=64)[:, n0 : n0 + nt],
-                in0=pkv_t[r][:, 0:nt, :].rearrange("p n (s c) -> p n s c", s=2),
-                in1=b_bc[:, P:OUT].rearrange("p (s c) -> p s c", s=2).unsqueeze(1).to_broadcast([P, nt, 2, 64]),
+                out=o[:, gn * 192 : gn * OUT].rearrange("p (n c) -> p n c", c=64)[:, n0 : n0 + nt, :],
+                in0=pn_t[r][:, 0:nt, 64:P],
+                in1=bb_nr[:, 64:P].unsqueeze(1).to_broadcast([P, nt, 64]),
                 op=ALU.add,
             )
 
-        def rope(g):
-            gn = sum([ROUNDS[j] for j in GROUPS[g]])
-            i0 = first[GROUPS[g][0]]
-            o = o_t[g]
-            cosv = cos_sb[:].rearrange("p (i c) -> p i c", c=32)[:, i0 : i0 + gn, :]
-            sinv = sin_sb[:].rearrange("p (i c) -> p i c", c=32)[:, i0 : i0 + gn, :]
-            t1q = spool.tile([P, GMAX * 64], F32)
-            t2q = spool.tile([P, GMAX * 64], F32)
-            t1k = spool.tile([P, GMAX * 32], F32)
-            t2k = spool.tile([P, GMAX * 32], F32)
-            xq = o[:, 0 : gn * P].rearrange("p (n h d) -> p n h d", h=2, d=64)
-            xk = o[:, gn * P : gn * 192].rearrange("p (n d) -> p n d", d=64)
-            t1qv = t1q[:, 0 : gn * 64].rearrange("p (n h c) -> p n h c", h=2, c=32)
-            t2qv = t2q[:, 0 : gn * 64].rearrange("p (n h c) -> p n h c", h=2, c=32)
-            t1kv = t1k[:, 0 : gn * 32].rearrange("p (n c) -> p n c", c=32)
-            t2kv = t2k[:, 0 : gn * 32].rearrange("p (n c) -> p n c", c=32)
-            nc.vector.tensor_tensor(
-                out=t1qv, in0=xq[:, :, :, 0:32], in1=cosv.unsqueeze(2).to_broadcast([P, gn, 2, 32]), op=ALU.mult
-            )
+        def rope_mul(r):
+            g = group_of[r]
+            nt = ROUNDS[r]
+            gn = gsize(g)
+            i0 = first[r]
+            n0 = first[r] - first[GROUPS[g][0]]
+            if r == GROUPS[g][0]:
+                t1 = spool.tile([P, 3 * GMAX * 32], F32)
+                t2 = spool.tile([P, 3 * GMAX * 32], F32)
+                t1_t[g] = t1
+                t2_t[g] = t2
+            t1v = t1_t[g][:].rearrange("p (h n c) -> p n h c", h=3, c=32)[:, n0 : n0 + nt]
+            t2v = t2_t[g][:].rearrange("p (h n c) -> p n h c", h=3, c=32)[:, n0 : n0 + nt]
+            cosv = cos_sb[:].rearrange("p (i c) -> p i c", c=32)[:, i0 : i0 + nt, :]
+            sinv = sin_sb[:].rearrange("p (i c) -> p i c", c=32)[:, i0 : i0 + nt, :]
+            xv = pb_t[r][:, 0:nt, 0:96].rearrange("p n (h c) -> p n h c", h=3)
+            nc.vector.tensor_tensor(out=t1v, in0=xv, in1=cosv.unsqueeze(2).to_broadcast([P, nt, 3, 32]), op=ALU.mult)
             for e in range(2):
                 lo, ot = 16 * e, 16 * (1 - e)
                 nc.vector.tensor_tensor(
-                    out=t2qv[:, :, :, lo : lo + 16],
-                    in0=xq[:, :, :, ot : ot + 16],
-                    in1=sinv[:, :, lo : lo + 16].unsqueeze(2).to_broadcast([P, gn, 2, 16]),
+                    out=t2v[:, :, :, lo : lo + 16],
+                    in0=xv[:, :, :, ot : ot + 16],
+                    in1=sinv[:, :, lo : lo + 16].unsqueeze(2).to_broadcast([P, nt, 3, 16]),
                     op=ALU.mult,
                 )
-            nc.vector.tensor_tensor(out=t1kv, in0=xk[:, :, 0:32], in1=cosv, op=ALU.mult)
-            for e in range(2):
-                lo, ot = 16 * e, 16 * (1 - e)
+            ku_out = o_t[g][:, gn * P : gn * 192].rearrange("p (n d) -> p n d", d=64)[:, n0 : n0 + nt, 32:64]
+            if KU_ON_SCALAR:
+                nc.scalar.copy(out=ku_out, in_=pb_t[r][:, 0:nt, 96:P])
+            else:
+                nc.vector.tensor_copy(out=ku_out, in_=pb_t[r][:, 0:nt, 96:P])
+
+        def rope_add(g):
+            gn = gsize(g)
+            o = o_t[g]
+            for h in range(3):
+                if h < 2:
+                    dst = o[:, 0 : gn * P].rearrange("p (n h d) -> p n h d", h=2, d=64)[:, :, h, 0:32]
+                else:
+                    dst = o[:, gn * P : gn * 192].rearrange("p (n d) -> p n d", d=64)[:, :, 0:32]
+                s0 = h * GMAX * 32
                 nc.vector.tensor_tensor(
-                    out=t2kv[:, :, lo : lo + 16], in0=xk[:, :, ot : ot + 16], in1=sinv[:, :, lo : lo + 16], op=ALU.mult
+                    out=dst.rearrange("p n (j e) -> p n j e", e=2),
+                    in0=t1_t[g][:, s0 : s0 + gn * 32].rearrange("p (n e j) -> p n j e", e=2, j=16),
+                    in1=t2_t[g][:, s0 : s0 + gn * 32].rearrange("p (n e j) -> p n j e", e=2, j=16),
+                    op=ALU.add,
                 )
-            add_eng = nc.gpsimd if g in GP_ADD else nc.vector
-            add_eng.tensor_tensor(
-                out=o[:, 0 : gn * P].rearrange("p (u d) -> p u d", d=64)[:, :, 0:32].rearrange("p u (j e) -> p u j e", e=2),
-                in0=t1q[:, 0 : gn * 64].rearrange("p (u e j) -> p u j e", e=2, j=16),
-                in1=t2q[:, 0 : gn * 64].rearrange("p (u e j) -> p u j e", e=2, j=16),
-                op=ALU.add,
-            )
-            add_eng.tensor_tensor(
-                out=xk[:, :, 0:32].rearrange("p u (j e) -> p u j e", e=2),
-                in0=t1k[:, 0 : gn * 32].rearrange("p (u e j) -> p u j e", e=2, j=16),
-                in1=t2k[:, 0 : gn * 32].rearrange("p (u e j) -> p u j e", e=2, j=16),
-                op=ALU.add,
-            )
 
         def store(g):
-            gn = sum([ROUNDS[j] for j in GROUPS[g]])
+            gn = gsize(g)
             i0 = first[GROUPS[g][0]]
             o = o_t[g]
-            nc.scalar.dma_start(out=q_v[:, i0 : i0 + gn, :], in_=o[:, 0 : gn * P].rearrange("p (n c) -> p n c", c=P))
-            nc.scalar.dma_start(
+            nc.sync.dma_start(out=q_v[:, i0 : i0 + gn, :], in_=o[:, 0 : gn * P].rearrange("p (n c) -> p n c", c=P))
+            nc.sync.dma_start(
                 out=k_v[:, i0 : i0 + gn, :], in_=o[:, gn * P : gn * 192].rearrange("p (n c) -> p n c", c=64)
             )
-            nc.scalar.dma_start(
+            nc.sync.dma_start(
                 out=v_v[:, i0 : i0 + gn, :], in_=o[:, gn * 192 : gn * OUT].rearrange("p (n c) -> p n c", c=64)
             )
 
@@ -198,6 +223,8 @@ def tile_selfattention_pa_t_kernel(tc, hidden_states, cos, sin, W_qkv, b_qkv, ou
         nc.vector.memset(b_row[:], 0.0)
         ones = const.tile([P, P], BF16)
         nc.vector.memset(ones[:], 1.0)
+        warm = const.tile([P, 1], F32)
+        nc.scalar.activation(out=warm[:], in_=ones[:, 0:1], func=ACT.Identity, scale=1.0)
 
         nc.sync.dma_start(out=b_row[0:1, :], in_=b_qkv.rearrange("(o c) -> o c", o=1))
         w_raw = const.tile([P, 2 * 4 * OUT], BF16)
@@ -207,26 +234,35 @@ def tile_selfattention_pa_t_kernel(tc, hidden_states, cos, sin, W_qkv, b_qkv, ou
         )
         sin_sb = const.tile([P, NT * 32], BF16)
         cos_sb = const.tile([P, NT * 32], BF16)
-        sin_v = sin.rearrange("(p i) c -> p (i c)", i=NT)
-        cos_v = cos.rearrange("(p i) c -> p (i c)", i=NT)
         for item in HEAD:
             if item[0] == "x":
                 load(int(item[1:]))
             else:
-                lo, hi = SC_PARTS[int(item[2:])]
-                nc.sync.dma_start(out=sin_sb[:, lo * 32 : hi * 32], in_=sin_v[:, lo * 32 : hi * 32])
-                nc.sync.dma_start(out=cos_sb[:, lo * 32 : hi * 32], in_=cos_v[:, lo * 32 : hi * 32])
+                nc.sync.dma_start(out=sin_sb[:], in_=sin.rearrange("(p i) c -> p (i c)", i=NT))
+                nc.sync.dma_start(out=cos_sb[:], in_=cos.rearrange("(p i) c -> p (i c)", i=NT))
 
-        pb = mm.tile([P, RMAX, P], F32, tag="pq")
-        pb2 = pb[:].rearrange("p a c -> p (a c)")[:, 0:OUT]
+        sneg = sin_sb[:].rearrange("p (i e j) -> p i e j", e=2, j=16)[:, :, 0, :]
+        nc.gpsimd.tensor_scalar(out=sneg, in0=sneg, scalar1=-1.0, scalar2=0.0, op0=ALU.mult, op1=ALU.add)
+
+        pbias = ps_n.tile([P, RMAX, P], F32, tag="pn")
+        pb2 = pbias[:].rearrange("p a c -> p (a c)")[:, 0:OUT]
         nc.tensor.matmul(out=pb2, lhsT=ones[:], rhs=b_row[:], start=True, stop=True)
-        b_bc = const.tile([P, OUT], F32)
         pbv = pb2.rearrange("p (n m) -> p n m", n=4)
-        bbv = b_bc[:].rearrange("p (n m) -> p n m", n=4)
+        bb_rp = const.tile([P, P], F32)
+        bb_nr = const.tile([P, P], F32)
         for e in range(2):
-            nc.scalar.copy(out=bbv[:, 0:3, 16 * e : 16 * e + 16], in_=pbv[:, 0:3, e:32:2])
-        nc.scalar.copy(out=bbv[:, 0:3, 32:64], in_=pbv[:, 0:3, 32:64])
-        nc.scalar.copy(out=bbv[:, 3, :], in_=pbv[:, 3, :])
+            nc.scalar.copy(
+                out=bb_rp[:, 0:96].rearrange("p (h c) -> p h c", h=3)[:, :, 16 * e : 16 * e + 16], in_=pbv[:, 0:3, e:32:2]
+            )
+        nc.scalar.copy(out=bb_rp[:, 96:P], in_=pbv[:, 2, 32:64])
+        nc.scalar.copy(out=bb_nr[:, 0:64].rearrange("p (h c) -> p h c", h=2), in_=pbv[:, 0:2, 32:64])
+        nc.scalar.copy(out=bb_nr[:, 64:P], in_=pbv[:, 3, :])
+        b_col = const.tile([P, 1], F32)
+
+        def bias_column():
+            pbt = ps_b.tile([P, RMAX, P], F32, tag="pb")
+            nc.tensor.transpose(pbt[:, 0, :], bb_rp[:], ident[:])
+            nc.scalar.copy(out=b_col[:], in_=pbt[:, 0, 0:1])
 
         w_codes, w_scl = [], []
 
@@ -234,48 +270,47 @@ def tile_selfattention_pa_t_kernel(tc, hidden_states, cos, sin, W_qkv, b_qkv, ou
             for g in range(2):
                 w_grp = const.tile([P, OUT * 4], BF16, name="w_grp%d" % g, align_bytes=64)
                 src = w_raw[:, g * 1024 : (g + 1) * 1024].rearrange("p (t n m) -> p n m t", t=4, n=4)
-                dst = w_grp[:].rearrange("p (n m t) -> p n m t", n=4, t=4)
                 for e in range(2):
-                    nc.vector.tensor_copy(out=dst[:, 0:3, 16 * e : 16 * e + 16, :], in_=src[:, 0:3, e:32:2, :])
-                nc.vector.tensor_copy(out=dst[:, 0:3, 32:64, :], in_=src[:, 0:3, 32:64, :])
-                nc.vector.tensor_copy(out=dst[:, 3, :, :], in_=src[:, 3, :, :])
+                    nc.vector.tensor_copy(
+                        out=w_grp[:, 0 : 96 * 4].rearrange("p (h m t) -> p h m t", h=3, t=4)[:, :, 16 * e : 16 * e + 16, :],
+                        in_=src[:, 0:3, e:32:2, :],
+                    )
+                nc.vector.tensor_copy(
+                    out=w_grp[:, 96 * 4 : P * 4].rearrange("p (m t) -> p m t", t=4), in_=src[:, 2, 32:64, :]
+                )
+                nc.vector.tensor_copy(
+                    out=w_grp[:, P * 4 : 192 * 4].rearrange("p (h m t) -> p h m t", h=2, t=4), in_=src[:, 0:2, 32:64, :]
+                )
+                nc.vector.tensor_copy(
+                    out=w_grp[:, 192 * 4 : OUT * 4].rearrange("p (m t) -> p m t", t=4), in_=src[:, 3, :, :]
+                )
                 wc = const.tile([P, OUT], U32, name="w_codes%d" % g, align_bytes=64)
                 ws = const.tile([P, OUT], U8, name="w_scl%d" % g, align_bytes=64)
                 nc.vector.quantize_mx(out=wc[:].bitcast(FP8X4), scales=ws[:], in_=w_grp[:])
                 w_codes.append(wc)
                 w_scl.append(ws)
 
-        negated = []
-
-        def negate_sin(g):
-            i0 = first[GROUPS[g][0]]
-            for part, (lo, hi) in enumerate(SC_PARTS):
-                if lo <= i0 < hi and part not in negated:
-                    negated.append(part)
-                    sneg = sin_sb[:, lo * 32 : hi * 32].rearrange("p (i e j) -> p i e j", e=2, j=16)[:, :, 0, :]
-                    nc.vector.tensor_scalar_mul(out=sneg, in0=sneg, scalar1=-1.0)
-
-        ng = len(GROUPS)
-        for g in range(-LT, ng + 1):
-            if g == -1:
+        for p in range(-2, nr + 1):
+            if 0 <= p + 2 < nr:
+                transp(p + 2)
+                if p + 2 + XB < nr:
+                    load(p + 2 + XB)
+                copyout(p + 2)
+            if p == -1:
+                bias_column()
                 w_prep()
-            if 0 <= g + 1 < ng:
-                for r in GROUPS[g + 1]:
-                    quant(r)
-            if 0 <= g - 1 < ng:
-                negate_sin(g - 1)
-                rope(g - 1)
-            if 0 <= g < ng:
-                for r in GROUPS[g]:
-                    bias_add(r)
-            if 0 <= g + 1 < ng:
-                for r in GROUPS[g + 1]:
-                    mx(r)
-            if 0 <= g + LT < ng:
-                for r in GROUPS[g + LT]:
-                    transp(r)
-                    if r + XB < nr:
-                        load(r + XB)
-                    copyout(r)
-            if 0 <= g - 1 < ng:
-                store(g - 1)
+            if 0 <= p + 1 < nr:
+                quant(p + 1)
+            if 0 <= p < nr:
+                bias_add(p)
+            if 0 <= p + 1 < nr:
+                mx(p + 1)
+                evac(p + 1)
+            if 0 <= p - 1 < nr:
+                rope_mul(p - 1)
+                g = group_of[p - 1]
+                if p - 1 == GROUPS[g][-1]:
+                    rope_add(g)
+                    store(g)
+            if 0 <= p < nr:
+                tback(p)

@@ -16,10 +16,10 @@ T, H, OUT = 8192, 1024, 256
 NT = T // P
 FLOPS = 2 * T * H * OUT
 
-ROUNDS = [2, 2] + [4] * 14 + [2, 2]
-GROUPS = [[0, 1]] + [[2 + 2 * g, 3 + 2 * g] for g in range(7)] + [[16], [17]]
-HEAD = ["x0", "x1", "x2", "x3", "sc", "x4", "x5", "x6", "x7"]
-XB = 8
+ROUNDS = [2, 2] + [4] * 13 + [2, 2, 2, 2]
+GROUPS = [[0, 1]] + [[2 + 2 * g, 3 + 2 * g] for g in range(6)] + [[14], [15, 16], [17], [18]]
+HEAD = ["x0", "x1", "x2", "x3", "sc", "x4", "x5"]
+XB = 6
 RMAX = 4
 GMAX = 8
 KU_ON_SCALAR = True
@@ -43,7 +43,7 @@ def tile_selfattention_pa_t_kernel(tc, hidden_states, cos, sin, W_qkv, b_qkv, ou
         const = ctx.enter_context(tc.tile_pool(name="const", bufs=1))
         xpool = ctx.enter_context(tc.tile_pool(name="xpool", bufs=XB))
         gpool = ctx.enter_context(tc.tile_pool(name="gpool", bufs=4))
-        opool = ctx.enter_context(tc.tile_pool(name="opool", bufs=4))
+        opool = ctx.enter_context(tc.tile_pool(name="opool", bufs=5))
         spool = ctx.enter_context(tc.tile_pool(name="spool", bufs=2))
         ps_x = ctx.enter_context(tc.psum_pool(name="ps_x", bufs=4))
         ps_n = ctx.enter_context(tc.psum_pool(name="ps_n", bufs=1))
@@ -241,8 +241,9 @@ def tile_selfattention_pa_t_kernel(tc, hidden_states, cos, sin, W_qkv, b_qkv, ou
                 nc.sync.dma_start(out=sin_sb[:], in_=sin.rearrange("(p i) c -> p (i c)", i=NT))
                 nc.sync.dma_start(out=cos_sb[:], in_=cos.rearrange("(p i) c -> p (i c)", i=NT))
 
-        sneg = sin_sb[:].rearrange("p (i e j) -> p i e j", e=2, j=16)[:, :, 0, :]
-        nc.gpsimd.tensor_scalar(out=sneg, in0=sneg, scalar1=-1.0, scalar2=0.0, op0=ALU.mult, op1=ALU.add)
+        for lo, hi in ((0, 8), (8, NT)):
+            sneg = sin_sb[:, lo * 32 : hi * 32].rearrange("p (i e j) -> p i e j", e=2, j=16)[:, :, 0, :]
+            nc.gpsimd.tensor_scalar(out=sneg, in0=sneg, scalar1=-1.0, scalar2=0.0, op0=ALU.mult, op1=ALU.add)
 
         pbias = ps_n.tile([P, RMAX, P], F32, tag="pn")
         pb2 = pbias[:].rearrange("p a c -> p (a c)")[:, 0:OUT]
@@ -267,28 +268,28 @@ def tile_selfattention_pa_t_kernel(tc, hidden_states, cos, sin, W_qkv, b_qkv, ou
         w_codes, w_scl = [], []
 
         def w_prep():
-            for g in range(2):
+            grouped = []
+            for g, copy in ((0, nc.vector.tensor_copy), (1, nc.scalar.copy)):
                 w_grp = const.tile([P, OUT * 4], BF16, name="w_grp%d" % g, align_bytes=64)
                 src = w_raw[:, g * 1024 : (g + 1) * 1024].rearrange("p (t n m) -> p n m t", t=4, n=4)
                 for e in range(2):
-                    nc.vector.tensor_copy(
+                    copy(
                         out=w_grp[:, 0 : 96 * 4].rearrange("p (h m t) -> p h m t", h=3, t=4)[:, :, 16 * e : 16 * e + 16, :],
                         in_=src[:, 0:3, e:32:2, :],
                     )
-                nc.vector.tensor_copy(
-                    out=w_grp[:, 96 * 4 : P * 4].rearrange("p (m t) -> p m t", t=4), in_=src[:, 2, 32:64, :]
-                )
-                nc.vector.tensor_copy(
-                    out=w_grp[:, P * 4 : 192 * 4].rearrange("p (h m t) -> p h m t", h=2, t=4), in_=src[:, 0:2, 32:64, :]
-                )
-                nc.vector.tensor_copy(
-                    out=w_grp[:, 192 * 4 : OUT * 4].rearrange("p (m t) -> p m t", t=4), in_=src[:, 3, :, :]
-                )
+                copy(out=w_grp[:, 96 * 4 : P * 4].rearrange("p (m t) -> p m t", t=4), in_=src[:, 2, 32:64, :])
+                copy(out=w_grp[:, P * 4 : 192 * 4].rearrange("p (h m t) -> p h m t", h=2, t=4), in_=src[:, 0:2, 32:64, :])
+                copy(out=w_grp[:, 192 * 4 : OUT * 4].rearrange("p (m t) -> p m t", t=4), in_=src[:, 3, :, :])
+                grouped.append(w_grp)
+            for g in range(2):
+                w_grp = grouped[g]
                 wc = const.tile([P, OUT], U32, name="w_codes%d" % g, align_bytes=64)
                 ws = const.tile([P, OUT], U8, name="w_scl%d" % g, align_bytes=64)
                 nc.vector.quantize_mx(out=wc[:].bitcast(FP8X4), scales=ws[:], in_=w_grp[:])
                 w_codes.append(wc)
                 w_scl.append(ws)
+
+        w_prep()
 
         for p in range(-2, nr + 1):
             if 0 <= p + 2 < nr:
@@ -298,7 +299,6 @@ def tile_selfattention_pa_t_kernel(tc, hidden_states, cos, sin, W_qkv, b_qkv, ou
                 copyout(p + 2)
             if p == -1:
                 bias_column()
-                w_prep()
             if 0 <= p + 1 < nr:
                 quant(p + 1)
             if 0 <= p < nr:

@@ -18,8 +18,8 @@ FLOPS = 2 * T * H * OUT
 
 ROUNDS = [2, 2] + [4] * 13 + [2, 2, 2, 2]
 GROUPS = [[0, 1]] + [[2 + 2 * g, 3 + 2 * g] for g in range(6)] + [[14], [15, 16], [17], [18]]
-HEAD = ["x0", "x1", "x2", "x3", "sc", "x4", "x5"]
-XB = 6
+HEAD = ["x0", "x1", "x2", "x3", "sc", "x4", "x5", "x6", "x7"]
+XB = 8
 RMAX = 4
 GMAX = 8
 KU_ON_SCALAR = True
@@ -268,28 +268,28 @@ def tile_selfattention_pa_t_kernel(tc, hidden_states, cos, sin, W_qkv, b_qkv, ou
         w_codes, w_scl = [], []
 
         def w_prep():
-            grouped = []
-            for g, copy in ((0, nc.vector.tensor_copy), (1, nc.scalar.copy)):
+            for g in range(2):
                 w_grp = const.tile([P, OUT * 4], BF16, name="w_grp%d" % g, align_bytes=64)
                 src = w_raw[:, g * 1024 : (g + 1) * 1024].rearrange("p (t n m) -> p n m t", t=4, n=4)
                 for e in range(2):
-                    copy(
+                    nc.vector.tensor_copy(
                         out=w_grp[:, 0 : 96 * 4].rearrange("p (h m t) -> p h m t", h=3, t=4)[:, :, 16 * e : 16 * e + 16, :],
                         in_=src[:, 0:3, e:32:2, :],
                     )
-                copy(out=w_grp[:, 96 * 4 : P * 4].rearrange("p (m t) -> p m t", t=4), in_=src[:, 2, 32:64, :])
-                copy(out=w_grp[:, P * 4 : 192 * 4].rearrange("p (h m t) -> p h m t", h=2, t=4), in_=src[:, 0:2, 32:64, :])
-                copy(out=w_grp[:, 192 * 4 : OUT * 4].rearrange("p (m t) -> p m t", t=4), in_=src[:, 3, :, :])
-                grouped.append(w_grp)
-            for g in range(2):
-                w_grp = grouped[g]
+                nc.vector.tensor_copy(
+                    out=w_grp[:, 96 * 4 : P * 4].rearrange("p (m t) -> p m t", t=4), in_=src[:, 2, 32:64, :]
+                )
+                nc.vector.tensor_copy(
+                    out=w_grp[:, P * 4 : 192 * 4].rearrange("p (h m t) -> p h m t", h=2, t=4), in_=src[:, 0:2, 32:64, :]
+                )
+                nc.vector.tensor_copy(
+                    out=w_grp[:, 192 * 4 : OUT * 4].rearrange("p (m t) -> p m t", t=4), in_=src[:, 3, :, :]
+                )
                 wc = const.tile([P, OUT], U32, name="w_codes%d" % g, align_bytes=64)
                 ws = const.tile([P, OUT], U8, name="w_scl%d" % g, align_bytes=64)
                 nc.vector.quantize_mx(out=wc[:].bitcast(FP8X4), scales=ws[:], in_=w_grp[:])
                 w_codes.append(wc)
                 w_scl.append(ws)
-
-        w_prep()
 
         for p in range(-2, nr + 1):
             if 0 <= p + 2 < nr:
@@ -299,6 +299,7 @@ def tile_selfattention_pa_t_kernel(tc, hidden_states, cos, sin, W_qkv, b_qkv, ou
                 copyout(p + 2)
             if p == -1:
                 bias_column()
+                w_prep()
             if 0 <= p + 1 < nr:
                 quant(p + 1)
             if 0 <= p < nr:

@@ -16,10 +16,10 @@ T, H, OUT = 8192, 1024, 256
 NT = T // P
 FLOPS = 2 * T * H * OUT
 
-ROUNDS = [2, 2] + [4] * 13 + [2, 2, 2, 2]
-GROUPS = [[0, 1]] + [[2 + 2 * g, 3 + 2 * g] for g in range(6)] + [[14], [15, 16], [17], [18]]
-HEAD = ["x0", "x1", "x2", "x3", "sc", "x4", "x5", "x6", "x7"]
-XB = 8
+ROUNDS = [2, 2] + [4] * 14 + [2, 2]
+GROUPS = [[0, 1]] + [[2 + 2 * g, 3 + 2 * g] for g in range(7)] + [[16], [17]]
+HEAD = ["x0", "x1", "x2", "x3", "sc", "x4", "x5"]
+XB = 6
 RMAX = 4
 GMAX = 8
 KU_ON_SCALAR = True
@@ -241,9 +241,8 @@ def tile_selfattention_pa_t_kernel(tc, hidden_states, cos, sin, W_qkv, b_qkv, ou
                 nc.sync.dma_start(out=sin_sb[:], in_=sin.rearrange("(p i) c -> p (i c)", i=NT))
                 nc.sync.dma_start(out=cos_sb[:], in_=cos.rearrange("(p i) c -> p (i c)", i=NT))
 
-        for lo, hi in ((0, 8), (8, NT)):
-            sneg = sin_sb[:, lo * 32 : hi * 32].rearrange("p (i e j) -> p i e j", e=2, j=16)[:, :, 0, :]
-            nc.gpsimd.tensor_scalar(out=sneg, in0=sneg, scalar1=-1.0, scalar2=0.0, op0=ALU.mult, op1=ALU.add)
+        sneg = sin_sb[:].rearrange("p (i e j) -> p i e j", e=2, j=16)[:, :, 0, :]
+        nc.gpsimd.tensor_scalar(out=sneg, in0=sneg, scalar1=-1.0, scalar2=0.0, op0=ALU.mult, op1=ALU.add)
 
         pbias = ps_n.tile([P, RMAX, P], F32, tag="pn")
         pb2 = pbias[:].rearrange("p a c -> p (a c)")[:, 0:OUT]
@@ -268,28 +267,28 @@ def tile_selfattention_pa_t_kernel(tc, hidden_states, cos, sin, W_qkv, b_qkv, ou
         w_codes, w_scl = [], []
 
         def w_prep():
-            for g in range(2):
+            grouped = []
+            for g, copy in ((0, nc.vector.tensor_copy), (1, nc.scalar.copy)):
                 w_grp = const.tile([P, OUT * 4], BF16, name="w_grp%d" % g, align_bytes=64)
                 src = w_raw[:, g * 1024 : (g + 1) * 1024].rearrange("p (t n m) -> p n m t", t=4, n=4)
                 for e in range(2):
-                    nc.vector.tensor_copy(
+                    copy(
                         out=w_grp[:, 0 : 96 * 4].rearrange("p (h m t) -> p h m t", h=3, t=4)[:, :, 16 * e : 16 * e + 16, :],
                         in_=src[:, 0:3, e:32:2, :],
                     )
-                nc.vector.tensor_copy(
-                    out=w_grp[:, 96 * 4 : P * 4].rearrange("p (m t) -> p m t", t=4), in_=src[:, 2, 32:64, :]
-                )
-                nc.vector.tensor_copy(
-                    out=w_grp[:, P * 4 : 192 * 4].rearrange("p (h m t) -> p h m t", h=2, t=4), in_=src[:, 0:2, 32:64, :]
-                )
-                nc.vector.tensor_copy(
-                    out=w_grp[:, 192 * 4 : OUT * 4].rearrange("p (m t) -> p m t", t=4), in_=src[:, 3, :, :]
-                )
+                copy(out=w_grp[:, 96 * 4 : P * 4].rearrange("p (m t) -> p m t", t=4), in_=src[:, 2, 32:64, :])
+                copy(out=w_grp[:, P * 4 : 192 * 4].rearrange("p (h m t) -> p h m t", h=2, t=4), in_=src[:, 0:2, 32:64, :])
+                copy(out=w_grp[:, 192 * 4 : OUT * 4].rearrange("p (m t) -> p m t", t=4), in_=src[:, 3, :, :])
+                grouped.append(w_grp)
+            for g in range(2):
+                w_grp = grouped[g]
                 wc = const.tile([P, OUT], U32, name="w_codes%d" % g, align_bytes=64)
                 ws = const.tile([P, OUT], U8, name="w_scl%d" % g, align_bytes=64)
                 nc.vector.quantize_mx(out=wc[:].bitcast(FP8X4), scales=ws[:], in_=w_grp[:])
                 w_codes.append(wc)
                 w_scl.append(ws)
+
+        w_prep()
 
         for p in range(-2, nr + 1):
             if 0 <= p + 2 < nr:
@@ -299,7 +298,6 @@ def tile_selfattention_pa_t_kernel(tc, hidden_states, cos, sin, W_qkv, b_qkv, ou
                 copyout(p + 2)
             if p == -1:
                 bias_column()
-                w_prep()
             if 0 <= p + 1 < nr:
                 quant(p + 1)
             if 0 <= p < nr:

from contextlib import ExitStack

import concourse.mybir as mybir
from concourse.masks import make_identity

F32 = mybir.dt.float32
BF16 = mybir.dt.bfloat16
U32 = mybir.dt.uint32
U8 = mybir.dt.uint8
FP8X4 = mybir.dt.float8_e4m3fn_x4
ALU = mybir.AluOpType
ACT = mybir.ActivationFunctionType

P = 128
T, H, OUT = 8192, 1024, 256
NT = T // P
FLOPS = 2 * T * H * OUT

ROUNDS = [2, 2] + [4] * 14 + [2, 2]
GROUPS = [[0, 1]] + [[2 + 2 * g, 3 + 2 * g] for g in range(7)] + [[16], [17]]
HEAD = ["x0", "x1", "x2", "x3", "sc", "x4", "x5"]
XB = 6
RMAX = 4
GMAX = 8
KU_ON_SCALAR = True


def tile_selfattention_pa_t_kernel(tc, hidden_states, cos, sin, W_qkv, b_qkv, out_0, out_1, out_2):
    nc = tc.nc
    nr = len(ROUNDS)
    first = [sum(ROUNDS[:r]) for r in range(nr)]
    group_of = {}
    for g, rs in enumerate(GROUPS):
        for r in rs:
            group_of[r] = g
    x_v = hidden_states.rearrange("(p i) k -> p i k", i=NT)
    q_v = out_0.rearrange("(p i) h d -> p i (h d)", i=NT)
    k_v = out_1.rearrange("(p i) h d -> p i (h d)", i=NT)
    v_v = out_2.rearrange("(p i) h d -> p i (h d)", i=NT)

    with ExitStack() as ctx:
        ctx.enter_context(tc.manual_schedule())
        const = ctx.enter_context(tc.tile_pool(name="const", bufs=1))
        xpool = ctx.enter_context(tc.tile_pool(name="xpool", bufs=XB))
        gpool = ctx.enter_context(tc.tile_pool(name="gpool", bufs=4))
        opool = ctx.enter_context(tc.tile_pool(name="opool", bufs=5))
        spool = ctx.enter_context(tc.tile_pool(name="spool", bufs=2))
        ps_x = ctx.enter_context(tc.psum_pool(name="ps_x", bufs=4))
        ps_n = ctx.enter_context(tc.psum_pool(name="ps_n", bufs=1))
        ps_t = ctx.enter_context(tc.psum_pool(name="ps_t", bufs=1))
        ps_b = ctx.enter_context(tc.psum_pool(name="ps_b", bufs=2))

        x_t, xt_t, grp_t, codes_t, scl_t, pn_t, pt_t, xr_t, pb_t, o_t, t1_t, t2_t = {}, {}, {}, {}, {}, {}, {}, {}, {}, {}, {}, {}

        def gsize(g):
            return sum([ROUNDS[j] for j in GROUPS[g]])

        def load(r):
            nt = ROUNDS[r]
            xc = xpool.tile([P, RMAX * H], BF16)
            nc.sync.dma_start(
                out=xc[:, 0 : nt * H].rearrange("p (n k) -> p n k", k=H),
                in_=x_v[:, first[r] : first[r] + nt, :],
            )
            x_t[r] = xc

        def transp(r):
            xw = x_t[r][:].bitcast(F32)
            xt_t[r] = []
            for a in range(ROUNDS[r]):
                xt = ps_x.tile([P, 4, P], F32)
                for b in range(4):
                    w0 = a * 512 + b * P
                    nc.tensor.transpose(xt[:, b, :], xw[:, w0 : w0 + P], ident[:])
                xt_t[r].append(xt)

        def copyout(r):
            nt = ROUNDS[r]
            grp = gpool.tile([P, RMAX * H], BF16, align_bytes=64)
            gw = grp[:].bitcast(F32)[:, 0 : nt * 512].rearrange("p (g a m u) -> p g a m u", g=2, a=nt, u=2)
            for a in range(nt):
                nc.scalar.copy(out=gw[:, :, a], in_=xt_t[r][a][:].rearrange("p (g u) m -> p g m u", u=2))
            grp_t[r] = grp

        def quant(r):
            nt = ROUNDS[r]
            codes = gpool.tile([P, RMAX * 256], U32, align_bytes=64)
            scl = gpool.tile([P, RMAX * 256], U8, align_bytes=64)
            nc.vector.quantize_mx(
                out=codes[:, 0 : nt * 256].bitcast(FP8X4),
                scales=scl[:, 0 : nt * 256],
                in_=grp_t[r][:, 0 : nt * H],
            )
            codes_t[r] = codes
            scl_t[r] = scl

        def mx(r):
            nt = ROUNDS[r]
            w = nt * P
            pt = ps_t.tile([P, RMAX * P], F32)
            for g in range(2):
                nc.tensor.matmul_mx(
                    out=pt[:, 0:w],
                    lhsT=w_codes[g][:, 0:P].bitcast(FP8X4),
                    lhsT_scale=w_scl[g][:, 0:P],
                    rhs=codes_t[r][:, g * w : (g + 1) * w].bitcast(FP8X4),
                    rhs_scale=scl_t[r][:, g * w : (g + 1) * w],
                    start=(g == 0),
                    stop=(g == 1),
                )
            pn = ps_n.tile([P, RMAX, P], F32)
            for a in range(nt):
                for g in range(2):
                    s0 = g * w + a * P
                    nc.tensor.matmul_mx(
                        out=pn[:, a, :],
                        lhsT=codes_t[r][:, s0 : s0 + P].bitcast(FP8X4),
                        lhsT_scale=scl_t[r][:, s0 : s0 + P],
                        rhs=w_codes[g][:, P:OUT].bitcast(FP8X4),
                        rhs_scale=w_scl[g][:, P:OUT],
                        start=(g == 0),
                        stop=(g == 1),
                    )
            pt_t[r] = pt
            pn_t[r] = pn

        def evac(r):
            w = ROUNDS[r] * P
            xr = spool.tile([P, RMAX * P], F32)
            nc.scalar.activation(out=xr[:, 0:w], in_=pt_t[r][:, 0:w], func=ACT.Identity, bias=b_col[:, 0:1], scale=1.0)
            xr_t[r] = xr

        def tback(r):
            pb = ps_b.tile([P, RMAX, P], F32)
            for a in range(ROUNDS[r]):
                nc.tensor.transpose(pb[:, a, :], xr_t[r][:, a * P : (a + 1) * P], ident[:])
            pb_t[r] = pb

        def bias_add(r):
            g = group_of[r]
            nt = ROUNDS[r]
            gn = gsize(g)
            n0 = first[r] - first[GROUPS[g][0]]
            if r == GROUPS[g][0]:
                o = opool.tile([P, GMAX * OUT], F32)
                o_t[g] = o
            o = o_t[g]
            nc.vector.tensor_tensor(
                out=o[:, 0 : gn * P].rearrange("p (n h d) -> p n h d", h=2, d=64)[:, n0 : n0 + nt, :, 32:64],
                in0=pn_t[r][:, 0:nt, 0:64].rearrange("p n (h c) -> p n h c", h=2),
                in1=bb_nr[:, 0:64].rearrange("p (h c) -> p h c", h=2).unsqueeze(1).to_broadcast([P, nt, 2, 32]),
                op=ALU.add,
            )
            nc.vector.tensor_tensor(
                out=o[:, gn * 192 : gn * OUT].rearrange("p (n c) -> p n c", c=64)[:, n0 : n0 + nt, :],
                in0=pn_t[r][:, 0:nt, 64:P],
                in1=bb_nr[:, 64:P].unsqueeze(1).to_broadcast([P, nt, 64]),
                op=ALU.add,
            )

        def rope_mul(r):
            g = group_of[r]
            nt = ROUNDS[r]
            gn = gsize(g)
            i0 = first[r]
            n0 = first[r] - first[GROUPS[g][0]]
            if r == GROUPS[g][0]:
                t1 = spool.tile([P, 3 * GMAX * 32], F32)
                t2 = spool.tile([P, 3 * GMAX * 32], F32)
                t1_t[g] = t1
                t2_t[g] = t2
            t1v = t1_t[g][:].rearrange("p (h n c) -> p n h c", h=3, c=32)[:, n0 : n0 + nt]
            t2v = t2_t[g][:].rearrange("p (h n c) -> p n h c", h=3, c=32)[:, n0 : n0 + nt]
            cosv = cos_sb[:].rearrange("p (i c) -> p i c", c=32)[:, i0 : i0 + nt, :]
            sinv = sin_sb[:].rearrange("p (i c) -> p i c", c=32)[:, i0 : i0 + nt, :]
            xv = pb_t[r][:, 0:nt, 0:96].rearrange("p n (h c) -> p n h c", h=3)
            nc.vector.tensor_tensor(out=t1v, in0=xv, in1=cosv.unsqueeze(2).to_broadcast([P, nt, 3, 32]), op=ALU.mult)
            for e in range(2):
                lo, ot = 16 * e, 16 * (1 - e)
                nc.vector.tensor_tensor(
                    out=t2v[:, :, :, lo : lo + 16],
                    in0=xv[:, :, :, ot : ot + 16],
                    in1=sinv[:, :, lo : lo + 16].unsqueeze(2).to_broadcast([P, nt, 3, 16]),
                    op=ALU.mult,
                )
            ku_out = o_t[g][:, gn * P : gn * 192].rearrange("p (n d) -> p n d", d=64)[:, n0 : n0 + nt, 32:64]
            if KU_ON_SCALAR:
                nc.scalar.copy(out=ku_out, in_=pb_t[r][:, 0:nt, 96:P])
            else:
                nc.vector.tensor_copy(out=ku_out, in_=pb_t[r][:, 0:nt, 96:P])

        def rope_add(g):
            gn = gsize(g)
            o = o_t[g]
            for h in range(3):
                if h < 2:
                    dst = o[:, 0 : gn * P].rearrange("p (n h d) -> p n h d", h=2, d=64)[:, :, h, 0:32]
                else:
                    dst = o[:, gn * P : gn * 192].rearrange("p (n d) -> p n d", d=64)[:, :, 0:32]
                s0 = h * GMAX * 32
                nc.vector.tensor_tensor(
                    out=dst.rearrange("p n (j e) -> p n j e", e=2),
                    in0=t1_t[g][:, s0 : s0 + gn * 32].rearrange("p (n e j) -> p n j e", e=2, j=16),
                    in1=t2_t[g][:, s0 : s0 + gn * 32].rearrange("p (n e j) -> p n j e", e=2, j=16),
                    op=ALU.add,
                )

        def store(g):
            gn = gsize(g)
            i0 = first[GROUPS[g][0]]
            o = o_t[g]
            nc.sync.dma_start(out=q_v[:, i0 : i0 + gn, :], in_=o[:, 0 : gn * P].rearrange("p (n c) -> p n c", c=P))
            nc.sync.dma_start(
                out=k_v[:, i0 : i0 + gn, :], in_=o[:, gn * P : gn * 192].rearrange("p (n c) -> p n c", c=64)
            )
            nc.sync.dma_start(
                out=v_v[:, i0 : i0 + gn, :], in_=o[:, gn * 192 : gn * OUT].rearrange("p (n c) -> p n c", c=64)
            )

        ident = const.tile([P, P], F32)
        make_identity(nc, ident[:])
        b_row = const.tile([P, OUT], BF16)
        nc.vector.memset(b_row[:], 0.0)
        ones = const.tile([P, P], BF16)
        nc.vector.memset(ones[:], 1.0)
        warm = const.tile([P, 1], F32)
        nc.scalar.activation(out=warm[:], in_=ones[:, 0:1], func=ACT.Identity, scale=1.0)

        nc.sync.dma_start(out=b_row[0:1, :], in_=b_qkv.rearrange("(o c) -> o c", o=1))
        w_raw = const.tile([P, 2 * 4 * OUT], BF16)
        nc.sync.dma_start(
            out=w_raw[:].rearrange("p (a f) -> p a f", a=4),
            in_=W_qkv.rearrange("(a p e) c -> p a (e c)", a=4, e=2),
        )
        sin_sb = const.tile([P, NT * 32], BF16)
        cos_sb = const.tile([P, NT * 32], BF16)
        for item in HEAD:
            if item[0] == "x":
                load(int(item[1:]))
            else:
                nc.sync.dma_start(out=sin_sb[:], in_=sin.rearrange("(p i) c -> p (i c)", i=NT))
                nc.sync.dma_start(out=cos_sb[:], in_=cos.rearrange("(p i) c -> p (i c)", i=NT))

        sneg = sin_sb[:].rearrange("p (i e j) -> p i e j", e=2, j=16)[:, :, 0, :]
        nc.gpsimd.tensor_scalar(out=sneg, in0=sneg, scalar1=-1.0, scalar2=0.0, op0=ALU.mult, op1=ALU.add)

        pbias = ps_n.tile([P, RMAX, P], F32, tag="pn")
        pb2 = pbias[:].rearrange("p a c -> p (a c)")[:, 0:OUT]
        nc.tensor.matmul(out=pb2, lhsT=ones[:], rhs=b_row[:], start=True, stop=True)
        pbv = pb2.rearrange("p (n m) -> p n m", n=4)
        bb_rp = const.tile([P, P], F32)
        bb_nr = const.tile([P, P], F32)
        for e in range(2):
            nc.scalar.copy(
                out=bb_rp[:, 0:96].rearrange("p (h c) -> p h c", h=3)[:, :, 16 * e : 16 * e + 16], in_=pbv[:, 0:3, e:32:2]
            )
        nc.scalar.copy(out=bb_rp[:, 96:P], in_=pbv[:, 2, 32:64])
        nc.scalar.copy(out=bb_nr[:, 0:64].rearrange("p (h c) -> p h c", h=2), in_=pbv[:, 0:2, 32:64])
        nc.scalar.copy(out=bb_nr[:, 64:P], in_=pbv[:, 3, :])
        b_col = const.tile([P, 1], F32)

        def bias_column():
            pbt = ps_b.tile([P, RMAX, P], F32, tag="pb")
            nc.tensor.transpose(pbt[:, 0, :], bb_rp[:], ident[:])
            nc.scalar.copy(out=b_col[:], in_=pbt[:, 0, 0:1])

        w_codes, w_scl = [], []

        def w_prep():
            grouped = []
            for g, copy in ((0, nc.vector.tensor_copy), (1, nc.scalar.copy)):
                w_grp = const.tile([P, OUT * 4], BF16, name="w_grp%d" % g, align_bytes=64)
                src = w_raw[:, g * 1024 : (g + 1) * 1024].rearrange("p (t n m) -> p n m t", t=4, n=4)
                for e in range(2):
                    copy(
                        out=w_grp[:, 0 : 96 * 4].rearrange("p (h m t) -> p h m t", h=3, t=4)[:, :, 16 * e : 16 * e + 16, :],
                        in_=src[:, 0:3, e:32:2, :],
                    )
                copy(out=w_grp[:, 96 * 4 : P * 4].rearrange("p (m t) -> p m t", t=4), in_=src[:, 2, 32:64, :])
                copy(out=w_grp[:, P * 4 : 192 * 4].rearrange("p (h m t) -> p h m t", h=2, t=4), in_=src[:, 0:2, 32:64, :])
                copy(out=w_grp[:, 192 * 4 : OUT * 4].rearrange("p (m t) -> p m t", t=4), in_=src[:, 3, :, :])
                grouped.append(w_grp)
            for g in range(2):
                w_grp = grouped[g]
                wc = const.tile([P, OUT], U32, name="w_codes%d" % g, align_bytes=64)
                ws = const.tile([P, OUT], U8, name="w_scl%d" % g, align_bytes=64)
                nc.vector.quantize_mx(out=wc[:].bitcast(FP8X4), scales=ws[:], in_=w_grp[:])
                w_codes.append(wc)
                w_scl.append(ws)

        w_prep()

        for p in range(-2, nr + 1):
            if 0 <= p + 2 < nr:
                transp(p + 2)
                if p + 2 + XB < nr:
                    load(p + 2 + XB)
                copyout(p + 2)
            if p == -1:
                bias_column()
            if 0 <= p + 1 < nr:
                quant(p + 1)
            if 0 <= p < nr:
                bias_add(p)
            if 0 <= p + 1 < nr:
                mx(p + 1)
                evac(p + 1)
            if 0 <= p - 1 < nr:
                rope_mul(p - 1)
                g = group_of[p - 1]
                if p - 1 == GROUPS[g][-1]:
                    rope_add(g)
                    store(g)
            if 0 <= p < nr:
                tback(p)
